import numpy as np
import ml_dtypes


def mxq(x, axis, fmt="e4m3"):
    dtype, down = {"e4m3": (ml_dtypes.float8_e4m3fn, 7), "e5m2": (ml_dtypes.float8_e5m2, 14)}[fmt]
    v = np.moveaxis(np.asarray(x, np.float32).astype(ml_dtypes.bfloat16).astype(np.float64), axis, -1)
    blocks = v.reshape(v.shape[:-1] + (-1, 32))
    amax = np.abs(blocks).max(-1, keepdims=True)
    byte = np.maximum(np.where(amax > 0, np.frexp(amax)[1] - 1 + 127, 0) - down, 1)
    scale = np.exp2(byte - 127.0)
    codes = (blocks / scale).astype(np.float32).astype(dtype).astype(np.float64)
    return np.moveaxis((codes * scale).reshape(v.shape), -1, axis)


WIDE = False


def mx_kscale(k):
    if not WIDE:
        return np.ones(k)
    levels = np.array([10, -10, 5, -5, 0])
    a = np.random.permutation(np.resize(levels, k // 512 * 4)).reshape(k // 512, 4)
    idx = np.arange(k)
    return np.exp2(a[idx // 512, idx % 128 // 32])


BF16 = ml_dtypes.bfloat16


def bf(x):
    return np.asarray(x, np.float32).astype(BF16)


def f64(x):
    return np.asarray(x).astype(np.float64)


B, C, CK, CV, CO, H, W, P1, P2, P3, P4 = 2, 512, 256, 256, 1024, 48, 48, 1, 3, 6, 8
EPS = 1e-5
N = H * W
CF = C + C


def bnrelu(x, gamma, beta, mean, var):
    inv = 1.0 / np.sqrt(var + EPS)
    return np.maximum((x - mean[None, :, None]) * (inv * gamma)[None, :, None] + beta[None, :, None], 0.0)


def setup_inputs():
    u = mx_kscale(CF)
    t, s = u[:C], u[C:]
    return {"ctx_attn": bf(np.random.standard_normal((B, CV, H, W)) * 0.4),
            "feats": bf(np.random.standard_normal((B, C, H, W)) * s[None, :, None, None]),
            "Ww": bf(np.random.standard_normal((C, CV)) * 2.5 / np.sqrt(CV) * t[:, None]),
            "bw": bf(np.random.standard_normal(C) * 0.2 * t),
            "Wo": bf(np.random.standard_normal((CO, CF)) / np.sqrt(CF) / u[None, :]),
            "bo": bf(np.random.standard_normal(CO) * 0.2),
            "go": bf(1.0 + 0.1 * np.random.standard_normal(CO)),
            "betao": bf(np.random.standard_normal(CO) * 0.2),
            "mo": bf(np.random.standard_normal(CO) * 0.2),
            "vo": bf(np.random.uniform(0.5, 1.5, CO))}


def reference(ctx_attn, feats, Ww, bw, Wo, bo, go, betao, mo, vo):
    ctx = f64(Ww) @ f64(ctx_attn).reshape(B, CV, N) + f64(bw)[None, :, None]
    fused = np.concatenate([ctx, f64(feats).reshape(B, C, N)], axis=1)
    y = (mxq(f64(Wo), 1, "e4m3") @ mxq(fused, 1, "e4m3")) + f64(bo)[None, :, None]
    return bnrelu(y, f64(go), f64(betao), f64(mo), f64(vo)).reshape(B, CO, H, W)

@@ -1,0 +1,224 @@
+from contextlib import ExitStack
+
+from concourse import mybir
+from concourse.masks import make_identity
+
+BF16 = mybir.dt.bfloat16
+F32 = mybir.dt.float32
+U32 = mybir.dt.uint32
+U8 = mybir.dt.uint8
+FP8X4 = mybir.dt.float8_e4m3fn_x4
+ACT = mybir.ActivationFunctionType
+ALU = mybir.AluOpType
+
+P = 128
+PACK = 4
+BATCH = 2
+CV = 256
+C = 512
+CO = 1024
+HW = 48 * 48
+EPS = 1e-5
+
+POSITIONS = BATCH * HW
+CHUNK = 512
+N_CHUNKS = POSITIONS // CHUNK
+SUB = 128
+SUBS = CHUNK // SUB
+K_TILES = CV // P
+PASSES = 2
+M_TILES = CO // P
+HALF = HW // 2
+LEAD = 3
+M_PER_STORE = 2
+
+FLOPS = 2 * POSITIONS * (C * CV + CO * 2 * C)
+
+
+def tile_apnb_pb_t_kernel(tc, ctx_attn, feats, Ww, bw, Wo, bo, go, betao, mo, vo, out):
+    nc = tc.nc
+    with ExitStack() as stack:
+        stack.enter_context(tc.manual_schedule())
+        keep = stack.enter_context(tc.tile_pool(name="keep", bufs=1))
+        wo_stage = stack.enter_context(tc.tile_pool(name="wo_stage", bufs=3))
+        grouped_pool = stack.enter_context(tc.tile_pool(name="grouped_pool", bufs=LEAD + 1))
+        fused_pool = stack.enter_context(tc.tile_pool(name="fused_pool", bufs=3))
+        y_pool = stack.enter_context(tc.tile_pool(name="y_pool", bufs=8))
+        ctx_psum = stack.enter_context(tc.psum_pool(name="ctx_psum", bufs=3))
+        y_psum = stack.enter_context(tc.psum_pool(name="y_psum", bufs=5))
+
+        ident_bf16 = keep.tile([P, P], BF16)
+        make_identity(nc, ident_bf16[:])
+        ident_f32 = keep.tile([P, P], F32)
+        make_identity(nc, ident_f32[:])
+
+        per_channel = {}
+        for name, vector in (("vo", vo), ("go", go), ("bo", bo), ("mo", mo), ("betao", betao)):
+            per_channel[name] = keep.tile([P, M_TILES], BF16, name=name + "_sb")
+            nc.scalar.dma_start(out=per_channel[name][:], in_=vector.rearrange("(p m) -> p m", m=M_TILES))
+        bw_sb = keep.tile([P, PACK], BF16)
+        nc.scalar.dma_start(
+            out=bw_sb[:].rearrange("p (u e) -> p u e", u=2), in_=bw.rearrange("(u p e) -> p u e", u=2, e=2)
+        )
+
+        ww_sb = keep.tile([P, PACK, CV], BF16)
+        a_sb = keep.tile([P, K_TILES, POSITIONS], BF16)
+        f_sb = keep.tile([P, PACK, POSITIONS], BF16)
+        wo_sb = keep.tile([P, M_TILES, 2 * C], BF16)
+
+        def load_ctx_attn(b, h):
+            cols = slice(h * HALF, (h + 1) * HALF)
+            nc.sync.dma_start(
+                out=a_sb[:, :, b * HW + h * HALF : b * HW + (h + 1) * HALF],
+                in_=ctx_attn[b].rearrange("(kt p) h w -> p kt (h w)", p=P)[:, :, cols],
+            )
+
+        def load_feats(b, h):
+            cols = slice(h * HALF, (h + 1) * HALF)
+            rows = feats[b].rearrange("(u p e) h w -> u p e (h w)", u=2, e=2)
+            for u in range(2):
+                nc.sync.dma_start(
+                    out=f_sb[:, 2 * u : 2 * u + 2, b * HW + h * HALF : b * HW + (h + 1) * HALF],
+                    in_=rows[u][:, :, cols],
+                )
+
+        nc.sync.dma_start(
+            out=ww_sb[:].rearrange("p (u e) k -> p u (e k)", u=2),
+            in_=Ww.rearrange("(u p e) k -> p u (e k)", u=2, e=2),
+        )
+        load_ctx_attn(0, 0)
+        load_feats(0, 0)
+        load_ctx_attn(0, 1)
+        wo_rows = Wo.rearrange("(p m) k -> p m k", m=M_TILES)
+        for m in range(0, M_TILES, 2):
+            nc.sync.dma_start(out=wo_sb[:, m : m + 2, :], in_=wo_rows[:, m : m + 2, :])
+        load_feats(0, 1)
+        for h in range(2):
+            load_ctx_attn(1, h)
+            load_feats(1, h)
+
+        gain = keep.tile([P, M_TILES], F32)
+        shift = keep.tile([P, M_TILES], F32)
+        nc.vector.tensor_scalar_add(out=gain[:], in0=per_channel["vo"][:], scalar1=EPS)
+        nc.scalar.sqrt(out=gain[:], in_=gain[:])
+        nc.vector.reciprocal(out=gain[:], in_=gain[:])
+        nc.vector.tensor_mul(out=gain[:], in0=gain[:], in1=per_channel["go"][:])
+        nc.vector.tensor_sub(out=shift[:], in0=per_channel["bo"][:], in1=per_channel["mo"][:])
+        nc.vector.tensor_mul(out=shift[:], in0=shift[:], in1=gain[:])
+        nc.vector.tensor_add(out=shift[:], in0=shift[:], in1=per_channel["betao"][:])
+
+        ww_t_ps = ctx_psum.tile([P, K_TILES, PACK, P], BF16, tag="ctx")
+        for kt in range(K_TILES):
+            for t in range(PACK):
+                nc.tensor.transpose(ww_t_ps[:, kt, t, :], ww_sb[:, t, kt * P : (kt + 1) * P], ident_bf16[:])
+        ww_t = keep.tile([P, K_TILES, PACK, P], BF16)
+        nc.scalar.copy(out=ww_t[:], in_=ww_t_ps[:])
+
+        grouped_of = {}
+        codes_of = {}
+        scales_of = {}
+
+        def compute_ctx(c):
+            grouped_of[c] = grouped_pool.tile([P, PASSES, CHUNK, PACK], BF16, name="grouped", align_bytes=64)
+            for s in range(SUBS):
+                first = c * CHUNK + s * SUB
+                ctx_ps = ctx_psum.tile([P, PACK, SUB], F32, tag="ctx")
+                for t in range(PACK):
+                    for kt in range(K_TILES):
+                        nc.tensor.matmul(
+                            out=ctx_ps[:, t, :],
+                            lhsT=ww_t[:, kt, t, :],
+                            rhs=a_sb[:, kt, first : first + SUB],
+                            start=(kt == 0),
+                            stop=(kt == K_TILES - 1),
+                        )
+                nc.vector.tensor_tensor(
+                    out=grouped_of[c][:, 0, s * SUB : (s + 1) * SUB, :],
+                    in0=ctx_ps[:].rearrange("p t n -> p n t"),
+                    in1=bw_sb[:].unsqueeze(1).to_broadcast([P, SUB, PACK]),
+                    op=ALU.add,
+                )
+
+        def regroup_feats(copy, c):
+            copy(
+                out=grouped_of[c][:, 1, :, :].rearrange("p (n i) t -> p n t i", i=4),
+                in_=f_sb[:, :, c * CHUNK : (c + 1) * CHUNK].rearrange("p t (n i) -> p n t i", i=4),
+            )
+
+        def quantise_fused(c):
+            codes_of[c] = fused_pool.tile([P, PASSES, CHUNK], U32, name="codes", align_bytes=64)
+            scales_of[c] = fused_pool.tile([P, PASSES, CHUNK], U8, name="scales", align_bytes=64)
+            nc.vector.quantize_mx(
+                out=codes_of[c][:].rearrange("p g n -> p (g n)").bitcast(FP8X4),
+                scales=scales_of[c][:].rearrange("p g n -> p (g n)"),
+                in_=grouped_of[c][:].rearrange("p g n t -> p (g n t)"),
+            )
+
+        wo_codes = keep.tile([P, M_TILES, PASSES, P], U32, align_bytes=64)
+        wo_scales = keep.tile([P, M_TILES, PASSES, P], U8, align_bytes=64)
+
+        def prepare_wo(m):
+            words = wo_sb[:, m, :].bitcast(F32)
+            wo_t_ps = y_psum.tile([P, PASSES * 2, P], F32, tag="y")
+            for gu in range(PASSES * 2):
+                nc.tensor.transpose(wo_t_ps[:, gu, :], words[:, gu * P : (gu + 1) * P], ident_f32[:])
+            wo_grouped = wo_stage.tile([P, PASSES, P, PACK], BF16, align_bytes=64)
+            nc.scalar.copy(
+                out=wo_grouped[:].bitcast(F32), in_=wo_t_ps[:].rearrange("p (g u) j -> p g j u", g=PASSES)
+            )
+            nc.vector.quantize_mx(
+                out=wo_codes[:, m, :, :].rearrange("p g j -> p (g j)").bitcast(FP8X4),
+                scales=wo_scales[:, m, :, :].rearrange("p g j -> p (g j)"),
+                in_=wo_grouped[:].rearrange("p g j t -> p (g j t)"),
+            )
+
+        out_rows = out.rearrange("b (p m) h w -> b p m (h w)", m=M_TILES)
+
+        def compute_out(c):
+            for m0 in range(0, M_TILES, M_PER_STORE):
+                y_sb = y_pool.tile([P, M_PER_STORE, CHUNK], F32)
+                for i in range(M_PER_STORE):
+                    m = m0 + i
+                    y_ps = y_psum.tile([P, CHUNK], F32, tag="y")
+                    for g in range(PASSES):
+                        nc.tensor.matmul_mx(
+                            out=y_ps[:],
+                            lhsT=wo_codes[:, m, g, :].bitcast(FP8X4),
+                            lhsT_scale=wo_scales[:, m, g, :],
+                            rhs=codes_of[c][:, g, :].bitcast(FP8X4),
+                            rhs_scale=scales_of[c][:, g, :],
+                            start=(g == 0),
+                            stop=(g == PASSES - 1),
+                        )
+                    nc.scalar.activation(
+                        out=y_sb[:, i, :],
+                        in_=y_ps[:],
+                        func=ACT.Relu,
+                        bias=shift[:, m : m + 1],
+                        scale=gain[:, m : m + 1],
+                    )
+                for b in range(BATCH):
+                    lo = max(c * CHUNK, b * HW)
+                    hi = min((c + 1) * CHUNK, (b + 1) * HW)
+                    if lo < hi:
+                        nc.sync.dma_start(
+                            out=out_rows[b][:, m0 : m0 + M_PER_STORE, lo - b * HW : hi - b * HW],
+                            in_=y_sb[:, :, lo - c * CHUNK : hi - c * CHUNK],
+                        )
+
+        for c in range(LEAD):
+            compute_ctx(c)
+        regroup_feats(nc.scalar.copy, 0)
+        regroup_feats(nc.scalar.copy, 1)
+        quantise_fused(0)
+        for m in range(M_TILES):
+            prepare_wo(m)
+
+        for c in range(N_CHUNKS):
+            if c + LEAD < N_CHUNKS:
+                compute_ctx(c + LEAD)
+            if c + 2 < N_CHUNKS:
+                regroup_feats(nc.vector.tensor_copy, c + 2)
+            if c + 1 < N_CHUNKS:
+                quantise_fused(c + 1)
+            compute_out(c)

@@ -28,11 +28,23 @@ SUBS = CHUNK // SUB
 K_TILES = CV // P
 PASSES = 2
 M_TILES = CO // P
-HALF = HW // 2
+PIECE_CHUNKS = 3
+PIECE = PIECE_CHUNKS * CHUNK
+N_PIECES = N_CHUNKS // PIECE_CHUNKS
 LEAD = 3
 M_PER_STORE = 2
 
 FLOPS = 2 * POSITIONS * (C * CV + CO * 2 * C)
+
+
+def batch_parts(lo, hi):
+    parts = []
+    for b in range(BATCH):
+        first = max(lo, b * HW)
+        end = min(hi, (b + 1) * HW)
+        if first < end:
+            parts.append((b, first - b * HW, end - b * HW, first - lo))
+    return parts
 
 
 def tile_apnb_pb_t_kernel(tc, ctx_attn, feats, Ww, bw, Wo, bo, go, betao, mo, vo, out):
@@ -62,40 +74,37 @@ def tile_apnb_pb_t_kernel(tc, ctx_attn, feats, Ww, bw, Wo, bo, go, betao, mo, vo
         )
 
         ww_sb = keep.tile([P, PACK, CV], BF16)
-        a_sb = keep.tile([P, K_TILES, POSITIONS], BF16)
-        f_sb = keep.tile([P, PACK, POSITIONS], BF16)
+        a_piece = [keep.tile([P, K_TILES, PIECE], BF16, name="a_piece%d" % j) for j in range(N_PIECES)]
+        f_piece = [keep.tile([P, PACK, PIECE], BF16, name="f_piece%d" % j) for j in range(N_PIECES)]
         wo_sb = keep.tile([P, M_TILES, 2 * C], BF16)
 
-        def load_ctx_attn(b, h):
-            cols = slice(h * HALF, (h + 1) * HALF)
-            nc.sync.dma_start(
-                out=a_sb[:, :, b * HW + h * HALF : b * HW + (h + 1) * HALF],
-                in_=ctx_attn[b].rearrange("(kt p) h w -> p kt (h w)", p=P)[:, :, cols],
-            )
-
-        def load_feats(b, h):
-            cols = slice(h * HALF, (h + 1) * HALF)
-            rows = feats[b].rearrange("(u p e) h w -> u p e (h w)", u=2, e=2)
-            for u in range(2):
+        def load_ctx_attn(j):
+            for b, first, end, at in batch_parts(j * PIECE, (j + 1) * PIECE):
                 nc.sync.dma_start(
-                    out=f_sb[:, 2 * u : 2 * u + 2, b * HW + h * HALF : b * HW + (h + 1) * HALF],
-                    in_=rows[u][:, :, cols],
+                    out=a_piece[j][:, :, at : at + end - first],
+                    in_=ctx_attn[b].rearrange("(kt p) h w -> p kt (h w)", p=P)[:, :, first:end],
                 )
+
+        def load_feats(j):
+            for b, first, end, at in batch_parts(j * PIECE, (j + 1) * PIECE):
+                rows = feats[b].rearrange("(u p e) h w -> u p e (h w)", u=2, e=2)
+                for u in range(2):
+                    nc.sync.dma_start(
+                        out=f_piece[j][:, 2 * u : 2 * u + 2, at : at + end - first], in_=rows[u][:, :, first:end]
+                    )
 
         nc.sync.dma_start(
             out=ww_sb[:].rearrange("p (u e) k -> p u (e k)", u=2),
             in_=Ww.rearrange("(u p e) k -> p u (e k)", u=2, e=2),
         )
-        load_ctx_attn(0, 0)
-        load_feats(0, 0)
-        load_ctx_attn(0, 1)
+        load_ctx_attn(0)
         wo_rows = Wo.rearrange("(p m) k -> p m k", m=M_TILES)
         for m in range(0, M_TILES, 2):
             nc.sync.dma_start(out=wo_sb[:, m : m + 2, :], in_=wo_rows[:, m : m + 2, :])
-        load_feats(0, 1)
-        for h in range(2):
-            load_ctx_attn(1, h)
-            load_feats(1, h)
+        load_feats(0)
+        for j in range(1, N_PIECES):
+            load_ctx_attn(j)
+            load_feats(j)
 
         gain = keep.tile([P, M_TILES], F32)
         shift = keep.tile([P, M_TILES], F32)
@@ -121,14 +130,14 @@ def tile_apnb_pb_t_kernel(tc, ctx_attn, feats, Ww, bw, Wo, bo, go, betao, mo, vo
         def compute_ctx(c):
             grouped_of[c] = grouped_pool.tile([P, PASSES, CHUNK, PACK], BF16, name="grouped", align_bytes=64)
             for s in range(SUBS):
-                first = c * CHUNK + s * SUB
+                first = (c % PIECE_CHUNKS) * CHUNK + s * SUB
                 ctx_ps = ctx_psum.tile([P, PACK, SUB], F32, tag="ctx")
                 for t in range(PACK):
                     for kt in range(K_TILES):
                         nc.tensor.matmul(
                             out=ctx_ps[:, t, :],
                             lhsT=ww_t[:, kt, t, :],
-                            rhs=a_sb[:, kt, first : first + SUB],
+                            rhs=a_piece[c // PIECE_CHUNKS][:, kt, first : first + SUB],
                             start=(kt == 0),
                             stop=(kt == K_TILES - 1),
                         )
@@ -140,9 +149,10 @@ def tile_apnb_pb_t_kernel(tc, ctx_attn, feats, Ww, bw, Wo, bo, go, betao, mo, vo
                 )
 
         def regroup_feats(copy, c):
+            first = (c % PIECE_CHUNKS) * CHUNK
             copy(
                 out=grouped_of[c][:, 1, :, :].rearrange("p (n i) t -> p n t i", i=4),
-                in_=f_sb[:, :, c * CHUNK : (c + 1) * CHUNK].rearrange("p t (n i) -> p n t i", i=4),
+                in_=f_piece[c // PIECE_CHUNKS][:, :, first : first + CHUNK].rearrange("p t (n i) -> p n t i", i=4),
             )
 
         def quantise_fused(c):
@@ -197,22 +207,19 @@ def tile_apnb_pb_t_kernel(tc, ctx_attn, feats, Ww, bw, Wo, bo, go, betao, mo, vo
                         bias=shift[:, m : m + 1],
                         scale=gain[:, m : m + 1],
                     )
-                for b in range(BATCH):
-                    lo = max(c * CHUNK, b * HW)
-                    hi = min((c + 1) * CHUNK, (b + 1) * HW)
-                    if lo < hi:
-                        nc.sync.dma_start(
-                            out=out_rows[b][:, m0 : m0 + M_PER_STORE, lo - b * HW : hi - b * HW],
-                            in_=y_sb[:, :, lo - c * CHUNK : hi - c * CHUNK],
-                        )
+                for b, first, end, at in batch_parts(c * CHUNK, (c + 1) * CHUNK):
+                    nc.sync.dma_start(
+                        out=out_rows[b][:, m0 : m0 + M_PER_STORE, first:end], in_=y_sb[:, :, at : at + end - first]
+                    )
 
-        for c in range(LEAD):
+        compute_ctx(0)
+        for m in range(M_TILES):
+            prepare_wo(m)
+        for c in range(1, LEAD):
             compute_ctx(c)
         regroup_feats(nc.scalar.copy, 0)
         regroup_feats(nc.scalar.copy, 1)
         quantise_fused(0)
-        for m in range(M_TILES):
-            prepare_wo(m)
 
         for c in range(N_CHUNKS):
             if c + LEAD < N_CHUNKS:

@@ -31,7 +31,9 @@ M_TILES = CO // P
 PIECE_CHUNKS = 3
 PIECE = PIECE_CHUNKS * CHUNK
 N_PIECES = N_CHUNKS // PIECE_CHUNKS
-LEAD = 3
+N_BANKS = POSITIONS // SUB
+HEAD_BANKS = 3 * SUBS
+ROUND_BANKS = (N_BANKS - HEAD_BANKS) // (N_CHUNKS - 1)
 M_PER_STORE = 2
 
 FLOPS = 2 * POSITIONS * (C * CV + CO * 2 * C)
@@ -53,7 +55,7 @@ def tile_apnb_pb_t_kernel(tc, ctx_attn, feats, Ww, bw, Wo, bo, go, betao, mo, vo
         stack.enter_context(tc.manual_schedule())
         keep = stack.enter_context(tc.tile_pool(name="keep", bufs=1))
         wo_stage = stack.enter_context(tc.tile_pool(name="wo_stage", bufs=3))
-        grouped_pool = stack.enter_context(tc.tile_pool(name="grouped_pool", bufs=LEAD + 1))
+        grouped_pool = stack.enter_context(tc.tile_pool(name="grouped_pool", bufs=HEAD_BANKS // SUBS + 1))
         fused_pool = stack.enter_context(tc.tile_pool(name="fused_pool", bufs=3))
         y_pool = stack.enter_context(tc.tile_pool(name="y_pool", bufs=8))
         ctx_psum = stack.enter_context(tc.psum_pool(name="ctx_psum", bufs=3))
@@ -127,26 +129,27 @@ def tile_apnb_pb_t_kernel(tc, ctx_attn, feats, Ww, bw, Wo, bo, go, betao, mo, vo
         codes_of = {}
         scales_of = {}
 
-        def compute_ctx(c):
-            grouped_of[c] = grouped_pool.tile([P, PASSES, CHUNK, PACK], BF16, name="grouped", align_bytes=64)
-            for s in range(SUBS):
-                first = (c % PIECE_CHUNKS) * CHUNK + s * SUB
-                ctx_ps = ctx_psum.tile([P, PACK, SUB], F32, tag="ctx")
-                for t in range(PACK):
-                    for kt in range(K_TILES):
-                        nc.tensor.matmul(
-                            out=ctx_ps[:, t, :],
-                            lhsT=ww_t[:, kt, t, :],
-                            rhs=a_piece[c // PIECE_CHUNKS][:, kt, first : first + SUB],
-                            start=(kt == 0),
-                            stop=(kt == K_TILES - 1),
-                        )
-                nc.vector.tensor_tensor(
-                    out=grouped_of[c][:, 0, s * SUB : (s + 1) * SUB, :],
-                    in0=ctx_ps[:].rearrange("p t n -> p n t"),
-                    in1=bw_sb[:].unsqueeze(1).to_broadcast([P, SUB, PACK]),
-                    op=ALU.add,
-                )
+        def compute_ctx_bank(j):
+            c, s = divmod(j, SUBS)
+            if s == 0:
+                grouped_of[c] = grouped_pool.tile([P, PASSES, CHUNK, PACK], BF16, name="grouped", align_bytes=64)
+            first = (c % PIECE_CHUNKS) * CHUNK + s * SUB
+            ctx_ps = ctx_psum.tile([P, PACK, SUB], F32, tag="ctx")
+            for t in range(PACK):
+                for kt in range(K_TILES):
+                    nc.tensor.matmul(
+                        out=ctx_ps[:, t, :],
+                        lhsT=ww_t[:, kt, t, :],
+                        rhs=a_piece[c // PIECE_CHUNKS][:, kt, first : first + SUB],
+                        start=(kt == 0),
+                        stop=(kt == K_TILES - 1),
+                    )
+            nc.vector.tensor_tensor(
+                out=grouped_of[c][:, 0, s * SUB : (s + 1) * SUB, :],
+                in0=ctx_ps[:].rearrange("p t n -> p n t"),
+                in1=bw_sb[:].unsqueeze(1).to_broadcast([P, SUB, PACK]),
+                op=ALU.add,
+            )
 
         def regroup_feats(copy, c):
             first = (c % PIECE_CHUNKS) * CHUNK
@@ -212,18 +215,19 @@ def tile_apnb_pb_t_kernel(tc, ctx_attn, feats, Ww, bw, Wo, bo, go, betao, mo, vo
                         out=out_rows[b][:, m0 : m0 + M_PER_STORE, first:end], in_=y_sb[:, :, at : at + end - first]
                     )
 
-        compute_ctx(0)
+        for j in range(SUBS):
+            compute_ctx_bank(j)
         for m in range(M_TILES):
             prepare_wo(m)
-        for c in range(1, LEAD):
-            compute_ctx(c)
+        for j in range(SUBS, HEAD_BANKS):
+            compute_ctx_bank(j)
         regroup_feats(nc.scalar.copy, 0)
         regroup_feats(nc.scalar.copy, 1)
         quantise_fused(0)
 
         for c in range(N_CHUNKS):
-            if c + LEAD < N_CHUNKS:
-                compute_ctx(c + LEAD)
+            for j in range(HEAD_BANKS + c * ROUND_BANKS, min(HEAD_BANKS + (c + 1) * ROUND_BANKS, N_BANKS)):
+                compute_ctx_bank(j)
             if c + 2 < N_CHUNKS:
                 regroup_feats(nc.vector.tensor_copy, c + 2)
             if c + 1 < N_CHUNKS:

@@ -34,7 +34,6 @@ N_PIECES = N_CHUNKS // PIECE_CHUNKS
 N_BANKS = POSITIONS // SUB
 HEAD_BANKS = 3 * SUBS
 ROUND_BANKS = (N_BANKS - HEAD_BANKS) // (N_CHUNKS - 1)
-M_PER_STORE = 2
 
 FLOPS = 2 * POSITIONS * (C * CV + CO * 2 * C)
 
@@ -57,7 +56,7 @@ def tile_apnb_pb_t_kernel(tc, ctx_attn, feats, Ww, bw, Wo, bo, go, betao, mo, vo
         wo_stage = stack.enter_context(tc.tile_pool(name="wo_stage", bufs=3))
         grouped_pool = stack.enter_context(tc.tile_pool(name="grouped_pool", bufs=HEAD_BANKS // SUBS + 1))
         fused_pool = stack.enter_context(tc.tile_pool(name="fused_pool", bufs=3))
-        y_pool = stack.enter_context(tc.tile_pool(name="y_pool", bufs=8))
+        y_pool = stack.enter_context(tc.tile_pool(name="y_pool", bufs=16))
         ctx_psum = stack.enter_context(tc.psum_pool(name="ctx_psum", bufs=3))
         y_psum = stack.enter_context(tc.psum_pool(name="y_psum", bufs=5))
 
@@ -100,10 +99,10 @@ def tile_apnb_pb_t_kernel(tc, ctx_attn, feats, Ww, bw, Wo, bo, go, betao, mo, vo
             in_=Ww.rearrange("(u p e) k -> p u (e k)", u=2, e=2),
         )
         load_ctx_attn(0)
+        load_feats(0)
         wo_rows = Wo.rearrange("(p m) k -> p m k", m=M_TILES)
         for m in range(0, M_TILES, 2):
             nc.sync.dma_start(out=wo_sb[:, m : m + 2, :], in_=wo_rows[:, m : m + 2, :])
-        load_feats(0)
         for j in range(1, N_PIECES):
             load_ctx_attn(j)
             load_feats(j)
@@ -188,42 +187,32 @@ def tile_apnb_pb_t_kernel(tc, ctx_attn, feats, Ww, bw, Wo, bo, go, betao, mo, vo
         out_rows = out.rearrange("b (p m) h w -> b p m (h w)", m=M_TILES)
 
         def compute_out(c):
-            for m0 in range(0, M_TILES, M_PER_STORE):
-                y_sb = y_pool.tile([P, M_PER_STORE, CHUNK], F32)
-                for i in range(M_PER_STORE):
-                    m = m0 + i
-                    y_ps = y_psum.tile([P, CHUNK], F32, tag="y")
-                    for g in range(PASSES):
-                        nc.tensor.matmul_mx(
-                            out=y_ps[:],
-                            lhsT=wo_codes[:, m, g, :].bitcast(FP8X4),
-                            lhsT_scale=wo_scales[:, m, g, :],
-                            rhs=codes_of[c][:, g, :].bitcast(FP8X4),
-                            rhs_scale=scales_of[c][:, g, :],
-                            start=(g == 0),
-                            stop=(g == PASSES - 1),
-                        )
-                    nc.scalar.activation(
-                        out=y_sb[:, i, :],
-                        in_=y_ps[:],
-                        func=ACT.Relu,
-                        bias=shift[:, m : m + 1],
-                        scale=gain[:, m : m + 1],
+            for m in range(M_TILES):
+                y_ps = y_psum.tile([P, CHUNK], F32, tag="y")
+                for g in range(PASSES):
+                    nc.tensor.matmul_mx(
+                        out=y_ps[:],
+                        lhsT=wo_codes[:, m, g, :].bitcast(FP8X4),
+                        lhsT_scale=wo_scales[:, m, g, :],
+                        rhs=codes_of[c][:, g, :].bitcast(FP8X4),
+                        rhs_scale=scales_of[c][:, g, :],
+                        start=(g == 0),
+                        stop=(g == PASSES - 1),
                     )
+                y_sb = y_pool.tile([P, CHUNK], F32)
+                nc.scalar.activation(
+                    out=y_sb[:], in_=y_ps[:], func=ACT.Relu, bias=shift[:, m : m + 1], scale=gain[:, m : m + 1]
+                )
                 for b, first, end, at in batch_parts(c * CHUNK, (c + 1) * CHUNK):
-                    nc.sync.dma_start(
-                        out=out_rows[b][:, m0 : m0 + M_PER_STORE, first:end], in_=y_sb[:, :, at : at + end - first]
-                    )
+                    nc.sync.dma_start(out=out_rows[b][:, m, first:end], in_=y_sb[:, at : at + end - first])
 
-        for j in range(SUBS):
-            compute_ctx_bank(j)
-        for m in range(M_TILES):
-            prepare_wo(m)
-        for j in range(SUBS, HEAD_BANKS):
+        for j in range(HEAD_BANKS):
             compute_ctx_bank(j)
         regroup_feats(nc.scalar.copy, 0)
         regroup_feats(nc.scalar.copy, 1)
         quantise_fused(0)
+        for m in range(M_TILES):
+            prepare_wo(m)
 
         for c in range(N_CHUNKS):
             for j in range(HEAD_BANKS + c * ROUND_BANKS, min(HEAD_BANKS + (c + 1) * ROUND_BANKS, N_BANKS)):

@@ -28,12 +28,11 @@ SUBS = CHUNK // SUB
 K_TILES = CV // P
 PASSES = 2
 M_TILES = CO // P
-PIECE_CHUNKS = 3
-PIECE = PIECE_CHUNKS * CHUNK
-N_PIECES = N_CHUNKS // PIECE_CHUNKS
+PIECES = ((0, 1), (1, 3), (3, 6), (6, 9))
+PIECE_OF = tuple(j for j, (first, end) in enumerate(PIECES) for c in range(first, end))
 N_BANKS = POSITIONS // SUB
-HEAD_BANKS = 3 * SUBS
-ROUND_BANKS = (N_BANKS - HEAD_BANKS) // (N_CHUNKS - 1)
+WARM_MATMULS = 5
+
 
 FLOPS = 2 * POSITIONS * (C * CV + CO * 2 * C)
 
@@ -54,7 +53,7 @@ def tile_apnb_pb_t_kernel(tc, ctx_attn, feats, Ww, bw, Wo, bo, go, betao, mo, vo
         stack.enter_context(tc.manual_schedule())
         keep = stack.enter_context(tc.tile_pool(name="keep", bufs=1))
         wo_stage = stack.enter_context(tc.tile_pool(name="wo_stage", bufs=3))
-        grouped_pool = stack.enter_context(tc.tile_pool(name="grouped_pool", bufs=HEAD_BANKS // SUBS + 1))
+        grouped_pool = stack.enter_context(tc.tile_pool(name="grouped_pool", bufs=4))
         fused_pool = stack.enter_context(tc.tile_pool(name="fused_pool", bufs=3))
         y_pool = stack.enter_context(tc.tile_pool(name="y_pool", bufs=16))
         ctx_psum = stack.enter_context(tc.psum_pool(name="ctx_psum", bufs=3))
@@ -65,29 +64,28 @@ def tile_apnb_pb_t_kernel(tc, ctx_attn, feats, Ww, bw, Wo, bo, go, betao, mo, vo
         ident_f32 = keep.tile([P, P], F32)
         make_identity(nc, ident_f32[:])
 
+        warm = keep.tile([P, 1], F32)
+        nc.vector.memset(warm[:], 1.0)
+        nc.scalar.activation(out=warm[:], in_=warm[:], func=ACT.Abs_reciprocal_sqrt)
         per_channel = {}
         for name, vector in (("vo", vo), ("go", go), ("bo", bo), ("mo", mo), ("betao", betao)):
             per_channel[name] = keep.tile([P, M_TILES], BF16, name=name + "_sb")
             nc.scalar.dma_start(out=per_channel[name][:], in_=vector.rearrange("(p m) -> p m", m=M_TILES))
-        bw_sb = keep.tile([P, PACK], BF16)
-        nc.scalar.dma_start(
-            out=bw_sb[:].rearrange("p (u e) -> p u e", u=2), in_=bw.rearrange("(u p e) -> p u e", u=2, e=2)
-        )
-
         ww_sb = keep.tile([P, PACK, CV], BF16)
-        a_piece = [keep.tile([P, K_TILES, PIECE], BF16, name="a_piece%d" % j) for j in range(N_PIECES)]
-        f_piece = [keep.tile([P, PACK, PIECE], BF16, name="f_piece%d" % j) for j in range(N_PIECES)]
+        width = [(end - first) * CHUNK for first, end in PIECES]
+        a_piece = [keep.tile([P, K_TILES, width[j]], BF16, name="a_piece%d" % j) for j in range(len(PIECES))]
+        f_piece = [keep.tile([P, PACK, width[j]], BF16, name="f_piece%d" % j) for j in range(len(PIECES))]
         wo_sb = keep.tile([P, M_TILES, 2 * C], BF16)
 
         def load_ctx_attn(j):
-            for b, first, end, at in batch_parts(j * PIECE, (j + 1) * PIECE):
+            for b, first, end, at in batch_parts(PIECES[j][0] * CHUNK, PIECES[j][1] * CHUNK):
                 nc.sync.dma_start(
                     out=a_piece[j][:, :, at : at + end - first],
                     in_=ctx_attn[b].rearrange("(kt p) h w -> p kt (h w)", p=P)[:, :, first:end],
                 )
 
         def load_feats(j):
-            for b, first, end, at in batch_parts(j * PIECE, (j + 1) * PIECE):
+            for b, first, end, at in batch_parts(PIECES[j][0] * CHUNK, PIECES[j][1] * CHUNK):
                 rows = feats[b].rearrange("(u p e) h w -> u p e (h w)", u=2, e=2)
                 for u in range(2):
                     nc.sync.dma_start(
@@ -98,48 +96,65 @@ def tile_apnb_pb_t_kernel(tc, ctx_attn, feats, Ww, bw, Wo, bo, go, betao, mo, vo
             out=ww_sb[:].rearrange("p (u e) k -> p u (e k)", u=2),
             in_=Ww.rearrange("(u p e) k -> p u (e k)", u=2, e=2),
         )
+        bw_sb = keep.tile([P, PACK], BF16)
+        nc.sync.dma_start(
+            out=bw_sb[:].rearrange("p (u e) -> p u e", u=2), in_=bw.rearrange("(u p e) -> p u e", u=2, e=2)
+        )
         load_ctx_attn(0)
         load_feats(0)
+        load_ctx_attn(1)
         wo_rows = Wo.rearrange("(p m) k -> p m k", m=M_TILES)
         for m in range(0, M_TILES, 2):
             nc.sync.dma_start(out=wo_sb[:, m : m + 2, :], in_=wo_rows[:, m : m + 2, :])
-        for j in range(1, N_PIECES):
+        load_feats(1)
+        for j in range(2, len(PIECES)):
             load_ctx_attn(j)
             load_feats(j)
 
+        zeros = keep.tile([P, CHUNK], BF16)
+        nc.vector.memset(zeros[:], 0.0)
+        idle_ps = y_psum.tile([P, CHUNK], F32, tag="y")
+        for i in range(WARM_MATMULS):
+            nc.tensor.matmul(out=idle_ps[:], lhsT=zeros[:, :P], rhs=zeros[:], start=True, stop=True)
+
+        ww_t = keep.tile([P, PACK, K_TILES, P], BF16)
+        for half in range(2):
+            ww_t_ps = ctx_psum.tile([P, PACK // 2, K_TILES, P], BF16, tag="ctx")
+            for i in range(PACK // 2):
+                for kt in range(K_TILES):
+                    nc.tensor.transpose(
+                        ww_t_ps[:, i, kt, :],
+                        ww_sb[:, half * PACK // 2 + i, kt * P : (kt + 1) * P],
+                        ident_bf16[:],
+                    )
+            nc.vector.tensor_copy(out=ww_t[:, half * PACK // 2 : (half + 1) * PACK // 2, :, :], in_=ww_t_ps[:])
+
         gain = keep.tile([P, M_TILES], F32)
         shift = keep.tile([P, M_TILES], F32)
-        nc.vector.tensor_scalar_add(out=gain[:], in0=per_channel["vo"][:], scalar1=EPS)
-        nc.scalar.sqrt(out=gain[:], in_=gain[:])
-        nc.vector.reciprocal(out=gain[:], in_=gain[:])
-        nc.vector.tensor_mul(out=gain[:], in0=gain[:], in1=per_channel["go"][:])
-        nc.vector.tensor_sub(out=shift[:], in0=per_channel["bo"][:], in1=per_channel["mo"][:])
-        nc.vector.tensor_mul(out=shift[:], in0=shift[:], in1=gain[:])
-        nc.vector.tensor_add(out=shift[:], in0=shift[:], in1=per_channel["betao"][:])
-
-        ww_t_ps = ctx_psum.tile([P, K_TILES, PACK, P], BF16, tag="ctx")
-        for kt in range(K_TILES):
-            for t in range(PACK):
-                nc.tensor.transpose(ww_t_ps[:, kt, t, :], ww_sb[:, t, kt * P : (kt + 1) * P], ident_bf16[:])
-        ww_t = keep.tile([P, K_TILES, PACK, P], BF16)
-        nc.scalar.copy(out=ww_t[:], in_=ww_t_ps[:])
+        nc.gpsimd.tensor_scalar_add(out=gain[:], in0=per_channel["vo"][:], scalar1=EPS)
+        nc.scalar.activation(out=gain[:], in_=gain[:], func=ACT.Abs_reciprocal_sqrt)
+        nc.gpsimd.tensor_mul(out=gain[:], in0=gain[:], in1=per_channel["go"][:])
+        nc.gpsimd.tensor_sub(out=shift[:], in0=per_channel["bo"][:], in1=per_channel["mo"][:])
+        nc.gpsimd.tensor_mul(out=shift[:], in0=shift[:], in1=gain[:])
+        nc.gpsimd.tensor_add(out=shift[:], in0=shift[:], in1=per_channel["betao"][:])
 
         grouped_of = {}
         codes_of = {}
         scales_of = {}
 
+        def new_grouped(c):
+            grouped_of[c] = grouped_pool.tile([P, PASSES, CHUNK, PACK], BF16, name="grouped", align_bytes=64)
+
         def compute_ctx_bank(j):
             c, s = divmod(j, SUBS)
-            if s == 0:
-                grouped_of[c] = grouped_pool.tile([P, PASSES, CHUNK, PACK], BF16, name="grouped", align_bytes=64)
-            first = (c % PIECE_CHUNKS) * CHUNK + s * SUB
+            first = (c - PIECES[PIECE_OF[c]][0]) * CHUNK + s * SUB
             ctx_ps = ctx_psum.tile([P, PACK, SUB], F32, tag="ctx")
             for t in range(PACK):
                 for kt in range(K_TILES):
                     nc.tensor.matmul(
                         out=ctx_ps[:, t, :],
-                        lhsT=ww_t[:, kt, t, :],
-                        rhs=a_piece[c // PIECE_CHUNKS][:, kt, first : first + SUB],
+                        lhsT=ww_t[:, t, kt, :],
+                        rhs=a_piece[PIECE_OF[c]][:, kt, first : first + SUB],
                         start=(kt == 0),
                         stop=(kt == K_TILES - 1),
                     )
@@ -151,19 +166,21 @@ def tile_apnb_pb_t_kernel(tc, ctx_attn, feats, Ww, bw, Wo, bo, go, betao, mo, vo
             )
 
         def regroup_feats(copy, c):
-            first = (c % PIECE_CHUNKS) * CHUNK
+            first = (c - PIECES[PIECE_OF[c]][0]) * CHUNK
             copy(
                 out=grouped_of[c][:, 1, :, :].rearrange("p (n i) t -> p n t i", i=4),
-                in_=f_piece[c // PIECE_CHUNKS][:, :, first : first + CHUNK].rearrange("p t (n i) -> p n t i", i=4),
+                in_=f_piece[PIECE_OF[c]][:, :, first : first + CHUNK].rearrange("p t (n i) -> p n t i", i=4),
             )
 
-        def quantise_fused(c):
+        def new_fused(c):
             codes_of[c] = fused_pool.tile([P, PASSES, CHUNK], U32, name="codes", align_bytes=64)
             scales_of[c] = fused_pool.tile([P, PASSES, CHUNK], U8, name="scales", align_bytes=64)
+
+        def quantise_fused(c, first=0, end=PASSES):
             nc.vector.quantize_mx(
-                out=codes_of[c][:].rearrange("p g n -> p (g n)").bitcast(FP8X4),
-                scales=scales_of[c][:].rearrange("p g n -> p (g n)"),
-                in_=grouped_of[c][:].rearrange("p g n t -> p (g n t)"),
+                out=codes_of[c][:, first:end, :].rearrange("p g n -> p (g n)").bitcast(FP8X4),
+                scales=scales_of[c][:, first:end, :].rearrange("p g n -> p (g n)"),
+                in_=grouped_of[c][:, first:end, :, :].rearrange("p g n t -> p (g n t)"),
             )
 
         wo_codes = keep.tile([P, M_TILES, PASSES, P], U32, align_bytes=64)
@@ -186,39 +203,55 @@ def tile_apnb_pb_t_kernel(tc, ctx_attn, feats, Ww, bw, Wo, bo, go, betao, mo, vo
 
         out_rows = out.rearrange("b (p m) h w -> b p m (h w)", m=M_TILES)
 
-        def compute_out(c):
-            for m in range(M_TILES):
-                y_ps = y_psum.tile([P, CHUNK], F32, tag="y")
-                for g in range(PASSES):
-                    nc.tensor.matmul_mx(
-                        out=y_ps[:],
-                        lhsT=wo_codes[:, m, g, :].bitcast(FP8X4),
-                        lhsT_scale=wo_scales[:, m, g, :],
-                        rhs=codes_of[c][:, g, :].bitcast(FP8X4),
-                        rhs_scale=scales_of[c][:, g, :],
-                        start=(g == 0),
-                        stop=(g == PASSES - 1),
-                    )
-                y_sb = y_pool.tile([P, CHUNK], F32)
-                nc.scalar.activation(
-                    out=y_sb[:], in_=y_ps[:], func=ACT.Relu, bias=shift[:, m : m + 1], scale=gain[:, m : m + 1]
+        def compute_out(c, m):
+            y_ps = y_psum.tile([P, CHUNK], F32, tag="y")
+            for g in range(PASSES):
+                nc.tensor.matmul_mx(
+                    out=y_ps[:],
+                    lhsT=wo_codes[:, m, g, :].bitcast(FP8X4),
+                    lhsT_scale=wo_scales[:, m, g, :],
+                    rhs=codes_of[c][:, g, :].bitcast(FP8X4),
+                    rhs_scale=scales_of[c][:, g, :],
+                    start=(g == 0),
+                    stop=(g == PASSES - 1),
                 )
-                for b, first, end, at in batch_parts(c * CHUNK, (c + 1) * CHUNK):
-                    nc.sync.dma_start(out=out_rows[b][:, m, first:end], in_=y_sb[:, at : at + end - first])
+            y_sb = y_pool.tile([P, CHUNK], F32)
+            nc.scalar.activation(
+                out=y_sb[:], in_=y_ps[:], func=ACT.Relu, bias=shift[:, m : m + 1], scale=gain[:, m : m + 1]
+            )
+            for b, first, end, at in batch_parts(c * CHUNK, (c + 1) * CHUNK):
+                nc.sync.dma_start(out=out_rows[b][:, m, first:end], in_=y_sb[:, at : at + end - first])
 
-        for j in range(HEAD_BANKS):
-            compute_ctx_bank(j)
+        new_grouped(0)
+        new_fused(0)
         regroup_feats(nc.scalar.copy, 0)
-        regroup_feats(nc.scalar.copy, 1)
-        quantise_fused(0)
-        for m in range(M_TILES):
-            prepare_wo(m)
+        for j in range(SUBS):
+            compute_ctx_bank(j)
+        quantise_fused(0, 1, 2)
+        quantise_fused(0, 0, 1)
+        new_grouped(1)
+        for i in range(SUBS):
+            prepare_wo(2 * i)
+            prepare_wo(2 * i + 1)
+            compute_ctx_bank(SUBS + i)
+        regroup_feats(nc.vector.tensor_copy, 1)
 
-        for c in range(N_CHUNKS):
-            for j in range(HEAD_BANKS + c * ROUND_BANKS, min(HEAD_BANKS + (c + 1) * ROUND_BANKS, N_BANKS)):
-                compute_ctx_bank(j)
-            if c + 2 < N_CHUNKS:
-                regroup_feats(nc.vector.tensor_copy, c + 2)
+        new_fused(1)
+        for m in range(M_TILES):
+            compute_out(0, m)
+            if m == M_TILES // 2:
+                quantise_fused(1)
+        new_grouped(2)
+        regroup_feats(nc.vector.tensor_copy, 2)
+
+        for c in range(1, N_CHUNKS):
             if c + 1 < N_CHUNKS:
+                new_fused(c + 1)
+                for j in range((c + 1) * SUBS, (c + 2) * SUBS):
+                    compute_ctx_bank(j)
                 quantise_fused(c + 1)
-            compute_out(c)
+            if c + 2 < N_CHUNKS:
+                new_grouped(c + 2)
+                regroup_feats(nc.vector.tensor_copy, c + 2)
+            for m in range(M_TILES):
+                compute_out(c, m)

@@ -55,9 +55,9 @@ def tile_apnb_pb_t_kernel(tc, ctx_attn, feats, Ww, bw, Wo, bo, go, betao, mo, vo
         wo_stage = stack.enter_context(tc.tile_pool(name="wo_stage", bufs=3))
         grouped_pool = stack.enter_context(tc.tile_pool(name="grouped_pool", bufs=4))
         fused_pool = stack.enter_context(tc.tile_pool(name="fused_pool", bufs=3))
-        y_pool = stack.enter_context(tc.tile_pool(name="y_pool", bufs=16))
-        ctx_psum = stack.enter_context(tc.psum_pool(name="ctx_psum", bufs=3))
-        y_psum = stack.enter_context(tc.psum_pool(name="y_psum", bufs=5))
+        y_pool = stack.enter_context(tc.tile_pool(name="y_pool", bufs=24))
+        ctx_psum = stack.enter_context(tc.psum_pool(name="ctx_psum", bufs=4))
+        y_psum = stack.enter_context(tc.psum_pool(name="y_psum", bufs=4))
 
         ident_bf16 = keep.tile([P, P], BF16)
         make_identity(nc, ident_bf16[:])

@@ -28,10 +28,19 @@ SUBS = CHUNK // SUB
 K_TILES = CV // P
 PASSES = 2
 M_TILES = CO // P
-PIECES = ((0, 1), (1, 3), (3, 6), (6, 9))
-PIECE_OF = tuple(j for j, (first, end) in enumerate(PIECES) for c in range(first, end))
-N_BANKS = POSITIONS // SUB
-WARM_MATMULS = 5
+VECTORS = 5
+PIECES = ((0, CHUNK), (CHUNK, 3 * CHUNK), (3 * CHUNK, HW), (HW, 2 * HW))
+
+
+def piece_parts(lo, hi):
+    parts = []
+    for j, (start, end) in enumerate(PIECES):
+        if max(lo, start) < min(hi, end):
+            parts.append((j, max(lo, start) - start, min(hi, end) - start, max(lo, start) - lo))
+    return parts
+
+
+WARM_MATMULS = 3
 
 
 FLOPS = 2 * POSITIONS * (C * CV + CO * 2 * C)
@@ -67,43 +76,46 @@ def tile_apnb_pb_t_kernel(tc, ctx_attn, feats, Ww, bw, Wo, bo, go, betao, mo, vo
         warm = keep.tile([P, 1], F32)
         nc.vector.memset(warm[:], 1.0)
         nc.scalar.activation(out=warm[:], in_=warm[:], func=ACT.Abs_reciprocal_sqrt)
-        per_channel = {}
-        for name, vector in (("vo", vo), ("go", go), ("bo", bo), ("mo", mo), ("betao", betao)):
-            per_channel[name] = keep.tile([P, M_TILES], BF16, name=name + "_sb")
-            nc.scalar.dma_start(out=per_channel[name][:], in_=vector.rearrange("(p m) -> p m", m=M_TILES))
+        vector_rows = keep.tile([P, P], BF16)
+        nc.vector.memset(vector_rows[:], 0.0)
+        for v, vector in enumerate((vo, go, bo, mo, betao)):
+            nc.scalar.dma_start(
+                out=vector_rows[v * M_TILES : (v + 1) * M_TILES, :], in_=vector.rearrange("(m p) -> m p", p=P)
+            )
+
         ww_sb = keep.tile([P, PACK, CV], BF16)
-        width = [(end - first) * CHUNK for first, end in PIECES]
+        width = [end - first for first, end in PIECES]
         a_piece = [keep.tile([P, K_TILES, width[j]], BF16, name="a_piece%d" % j) for j in range(len(PIECES))]
         f_piece = [keep.tile([P, PACK, width[j]], BF16, name="f_piece%d" % j) for j in range(len(PIECES))]
         wo_sb = keep.tile([P, M_TILES, 2 * C], BF16)
 
         def load_ctx_attn(j):
-            for b, first, end, at in batch_parts(PIECES[j][0] * CHUNK, PIECES[j][1] * CHUNK):
-                nc.sync.dma_start(
-                    out=a_piece[j][:, :, at : at + end - first],
-                    in_=ctx_attn[b].rearrange("(kt p) h w -> p kt (h w)", p=P)[:, :, first:end],
-                )
+            b, first = divmod(PIECES[j][0], HW)
+            nc.sync.dma_start(
+                out=a_piece[j][:],
+                in_=ctx_attn[b].rearrange("(kt p) h w -> p kt (h w)", p=P)[:, :, first : first + width[j]],
+            )
 
         def load_feats(j):
-            for b, first, end, at in batch_parts(PIECES[j][0] * CHUNK, PIECES[j][1] * CHUNK):
-                rows = feats[b].rearrange("(u p e) h w -> u p e (h w)", u=2, e=2)
-                for u in range(2):
-                    nc.sync.dma_start(
-                        out=f_piece[j][:, 2 * u : 2 * u + 2, at : at + end - first], in_=rows[u][:, :, first:end]
-                    )
+            b, first = divmod(PIECES[j][0], HW)
+            rows = feats[b].rearrange("(u p e) h w -> u p e (h w)", u=2, e=2)
+            for u in range(2):
+                nc.sync.dma_start(
+                    out=f_piece[j][:, 2 * u : 2 * u + 2, :], in_=rows[u][:, :, first : first + width[j]]
+                )
 
         nc.sync.dma_start(
             out=ww_sb[:].rearrange("p (u e) k -> p u (e k)", u=2),
             in_=Ww.rearrange("(u p e) k -> p u (e k)", u=2, e=2),
         )
+        load_ctx_attn(0)
         bw_sb = keep.tile([P, PACK], BF16)
         nc.sync.dma_start(
             out=bw_sb[:].rearrange("p (u e) -> p u e", u=2), in_=bw.rearrange("(u p e) -> p u e", u=2, e=2)
         )
-        load_ctx_attn(0)
         load_feats(0)
         load_ctx_attn(1)
-        wo_rows = Wo.rearrange("(p m) k -> p m k", m=M_TILES)
+        wo_rows = Wo.rearrange("(m p) k -> p m k", p=P)
         for m in range(0, M_TILES, 2):
             nc.sync.dma_start(out=wo_sb[:, m : m + 2, :], in_=wo_rows[:, m : m + 2, :])
         load_feats(1)
@@ -129,15 +141,6 @@ def tile_apnb_pb_t_kernel(tc, ctx_attn, feats, Ww, bw, Wo, bo, go, betao, mo, vo
                     )
             nc.vector.tensor_copy(out=ww_t[:, half * PACK // 2 : (half + 1) * PACK // 2, :, :], in_=ww_t_ps[:])
 
-        gain = keep.tile([P, M_TILES], F32)
-        shift = keep.tile([P, M_TILES], F32)
-        nc.gpsimd.tensor_scalar_add(out=gain[:], in0=per_channel["vo"][:], scalar1=EPS)
-        nc.scalar.activation(out=gain[:], in_=gain[:], func=ACT.Abs_reciprocal_sqrt)
-        nc.gpsimd.tensor_mul(out=gain[:], in0=gain[:], in1=per_channel["go"][:])
-        nc.gpsimd.tensor_sub(out=shift[:], in0=per_channel["bo"][:], in1=per_channel["mo"][:])
-        nc.gpsimd.tensor_mul(out=shift[:], in0=shift[:], in1=gain[:])
-        nc.gpsimd.tensor_add(out=shift[:], in0=shift[:], in1=per_channel["betao"][:])
-
         grouped_of = {}
         codes_of = {}
         scales_of = {}
@@ -147,14 +150,14 @@ def tile_apnb_pb_t_kernel(tc, ctx_attn, feats, Ww, bw, Wo, bo, go, betao, mo, vo
 
         def compute_ctx_bank(j):
             c, s = divmod(j, SUBS)
-            first = (c - PIECES[PIECE_OF[c]][0]) * CHUNK + s * SUB
+            ((piece, first, end, at),) = piece_parts(j * SUB, (j + 1) * SUB)
             ctx_ps = ctx_psum.tile([P, PACK, SUB], F32, tag="ctx")
             for t in range(PACK):
                 for kt in range(K_TILES):
                     nc.tensor.matmul(
                         out=ctx_ps[:, t, :],
                         lhsT=ww_t[:, t, kt, :],
-                        rhs=a_piece[PIECE_OF[c]][:, kt, first : first + SUB],
+                        rhs=a_piece[piece][:, kt, first:end],
                         start=(kt == 0),
                         stop=(kt == K_TILES - 1),
                     )
@@ -166,11 +169,11 @@ def tile_apnb_pb_t_kernel(tc, ctx_attn, feats, Ww, bw, Wo, bo, go, betao, mo, vo
             )
 
         def regroup_feats(copy, c):
-            first = (c - PIECES[PIECE_OF[c]][0]) * CHUNK
-            copy(
-                out=grouped_of[c][:, 1, :, :].rearrange("p (n i) t -> p n t i", i=4),
-                in_=f_piece[PIECE_OF[c]][:, :, first : first + CHUNK].rearrange("p t (n i) -> p n t i", i=4),
-            )
+            for piece, first, end, at in piece_parts(c * CHUNK, (c + 1) * CHUNK):
+                copy(
+                    out=grouped_of[c][:, 1, at : at + end - first, :].rearrange("p (n i) t -> p n t i", i=4),
+                    in_=f_piece[piece][:, :, first:end].rearrange("p t (n i) -> p n t i", i=4),
+                )
 
         def new_fused(c):
             codes_of[c] = fused_pool.tile([P, PASSES, CHUNK], U32, name="codes", align_bytes=64)
@@ -201,7 +204,7 @@ def tile_apnb_pb_t_kernel(tc, ctx_attn, feats, Ww, bw, Wo, bo, go, betao, mo, vo
                 in_=wo_grouped[:].rearrange("p g j t -> p (g j t)"),
             )
 
-        out_rows = out.rearrange("b (p m) h w -> b p m (h w)", m=M_TILES)
+        out_rows = out.rearrange("b (m p) h w -> b p m (h w)", p=P)
 
         def compute_out(c, m):
             y_ps = y_psum.tile([P, CHUNK], F32, tag="y")
@@ -227,6 +230,24 @@ def tile_apnb_pb_t_kernel(tc, ctx_attn, feats, Ww, bw, Wo, bo, go, betao, mo, vo
         regroup_feats(nc.scalar.copy, 0)
         for j in range(SUBS):
             compute_ctx_bank(j)
+
+        columns_ps = ctx_psum.tile([P, P], BF16, tag="ctx")
+        nc.tensor.transpose(columns_ps[:], vector_rows[:], ident_bf16[:])
+        columns = keep.tile([P, VECTORS, M_TILES], F32)
+        nc.vector.tensor_copy(
+            out=columns[:].rearrange("p v m -> p (v m)"), in_=columns_ps[:, : VECTORS * M_TILES]
+        )
+        gain = keep.tile([P, M_TILES], F32)
+        shift = keep.tile([P, M_TILES], F32)
+        nc.gpsimd.tensor_scalar_add(out=gain[:], in0=columns[:, 0, :], scalar1=EPS)
+        nc.gpsimd.tensor_sub(out=shift[:], in0=columns[:, 2, :], in1=columns[:, 3, :])
+
+        def finish_norm():
+            nc.scalar.activation(out=gain[:], in_=gain[:], func=ACT.Abs_reciprocal_sqrt)
+            nc.gpsimd.tensor_mul(out=gain[:], in0=gain[:], in1=columns[:, 1, :])
+            nc.gpsimd.tensor_mul(out=shift[:], in0=shift[:], in1=gain[:])
+            nc.gpsimd.tensor_add(out=shift[:], in0=shift[:], in1=columns[:, 4, :])
+
         quantise_fused(0, 1, 2)
         quantise_fused(0, 0, 1)
         new_grouped(1)
@@ -234,6 +255,8 @@ def tile_apnb_pb_t_kernel(tc, ctx_attn, feats, Ww, bw, Wo, bo, go, betao, mo, vo
             prepare_wo(2 * i)
             prepare_wo(2 * i + 1)
             compute_ctx_bank(SUBS + i)
+            if i == 1:
+                finish_norm()
         regroup_feats(nc.vector.tensor_copy, 1)
 
         new_fused(1)

@@ -28,7 +28,10 @@ SUBS = CHUNK // SUB
 K_TILES = CV // P
 PASSES = 2
 M_TILES = CO // P
-VECTORS = 5
+PAIR = 2
+M_PAIRS = M_TILES // PAIR
+N_BANKS = POSITIONS // SUB
+HEAD_BANKS = 10
 PIECES = ((0, CHUNK), (CHUNK, 3 * CHUNK), (3 * CHUNK, HW), (HW, 2 * HW))
 
 
@@ -41,6 +44,10 @@ def piece_parts(lo, hi):
 
 
 WARM_MATMULS = 3
+
+
+def banks_by(c):
+    return min(N_BANKS, HEAD_BANKS + -(-c * (N_BANKS - HEAD_BANKS) // (N_CHUNKS - 2)))
 
 
 FLOPS = 2 * POSITIONS * (C * CV + CO * 2 * C)
@@ -76,13 +83,10 @@ def tile_apnb_pb_t_kernel(tc, ctx_attn, feats, Ww, bw, Wo, bo, go, betao, mo, vo
         warm = keep.tile([P, 1], F32)
         nc.vector.memset(warm[:], 1.0)
         nc.scalar.activation(out=warm[:], in_=warm[:], func=ACT.Abs_reciprocal_sqrt)
-        vector_rows = keep.tile([P, P], BF16)
-        nc.vector.memset(vector_rows[:], 0.0)
-        for v, vector in enumerate((vo, go, bo, mo, betao)):
-            nc.scalar.dma_start(
-                out=vector_rows[v * M_TILES : (v + 1) * M_TILES, :], in_=vector.rearrange("(m p) -> m p", p=P)
-            )
-
+        bw_rows = keep.tile([P, PAIR * P], BF16)
+        nc.vector.memset(bw_rows[:], 0.0)
+        vector_rows = keep.tile([P, PAIR * P], BF16)
+        nc.gpsimd.memset(vector_rows[:], 0.0)
         ww_sb = keep.tile([P, PACK, CV], BF16)
         width = [end - first for first, end in PIECES]
         a_piece = [keep.tile([P, K_TILES, width[j]], BF16, name="a_piece%d" % j) for j in range(len(PIECES))]
@@ -108,16 +112,21 @@ def tile_apnb_pb_t_kernel(tc, ctx_attn, feats, Ww, bw, Wo, bo, go, betao, mo, vo
             out=ww_sb[:].rearrange("p (u e) k -> p u (e k)", u=2),
             in_=Ww.rearrange("(u p e) k -> p u (e k)", u=2, e=2),
         )
+        nc.sync.dma_start(out=bw_rows[:2, :], in_=bw.rearrange("(u w) -> u w", u=2))
         load_ctx_attn(0)
-        bw_sb = keep.tile([P, PACK], BF16)
-        nc.sync.dma_start(
-            out=bw_sb[:].rearrange("p (u e) -> p u e", u=2), in_=bw.rearrange("(u p e) -> p u e", u=2, e=2)
-        )
         load_feats(0)
         load_ctx_attn(1)
-        wo_rows = Wo.rearrange("(m p) k -> p m k", p=P)
-        for m in range(0, M_TILES, 2):
-            nc.sync.dma_start(out=wo_sb[:, m : m + 2, :], in_=wo_rows[:, m : m + 2, :])
+        for i in range(M_PAIRS):
+            if i == 2:
+                for v, vector in enumerate((vo, go, bo, mo, betao)):
+                    nc.sync.dma_start(
+                        out=vector_rows[v * M_PAIRS : (v + 1) * M_PAIRS, :],
+                        in_=vector.rearrange("(i w) -> i w", i=M_PAIRS),
+                    )
+            nc.sync.dma_start(
+                out=wo_sb[:, PAIR * i : PAIR * (i + 1), :].rearrange("p e k -> p (e k)"),
+                in_=Wo[PAIR * P * i : PAIR * P * (i + 1), :].rearrange("(p e) k -> p (e k)", e=PAIR),
+            )
         load_feats(1)
         for j in range(2, len(PIECES)):
             load_ctx_attn(j)
@@ -145,8 +154,10 @@ def tile_apnb_pb_t_kernel(tc, ctx_attn, feats, Ww, bw, Wo, bo, go, betao, mo, vo
         codes_of = {}
         scales_of = {}
 
-        def new_grouped(c):
-            grouped_of[c] = grouped_pool.tile([P, PASSES, CHUNK, PACK], BF16, name="grouped", align_bytes=64)
+        def grouped(c):
+            if c not in grouped_of:
+                grouped_of[c] = grouped_pool.tile([P, PASSES, CHUNK, PACK], BF16, name="grouped", align_bytes=64)
+            return grouped_of[c]
 
         def compute_ctx_bank(j):
             c, s = divmod(j, SUBS)
@@ -162,16 +173,16 @@ def tile_apnb_pb_t_kernel(tc, ctx_attn, feats, Ww, bw, Wo, bo, go, betao, mo, vo
                         stop=(kt == K_TILES - 1),
                     )
             nc.vector.tensor_tensor(
-                out=grouped_of[c][:, 0, s * SUB : (s + 1) * SUB, :],
+                out=grouped(c)[:, 0, s * SUB : (s + 1) * SUB, :],
                 in0=ctx_ps[:].rearrange("p t n -> p n t"),
-                in1=bw_sb[:].unsqueeze(1).to_broadcast([P, SUB, PACK]),
+                in1=bw_sb.unsqueeze(1).to_broadcast([P, SUB, PACK]),
                 op=ALU.add,
             )
 
         def regroup_feats(copy, c):
             for piece, first, end, at in piece_parts(c * CHUNK, (c + 1) * CHUNK):
                 copy(
-                    out=grouped_of[c][:, 1, at : at + end - first, :].rearrange("p (n i) t -> p n t i", i=4),
+                    out=grouped(c)[:, 1, at : at + end - first, :].rearrange("p (n i) t -> p n t i", i=4),
                     in_=f_piece[piece][:, :, first:end].rearrange("p t (n i) -> p n t i", i=4),
                 )
 
@@ -204,7 +215,7 @@ def tile_apnb_pb_t_kernel(tc, ctx_attn, feats, Ww, bw, Wo, bo, go, betao, mo, vo
                 in_=wo_grouped[:].rearrange("p g j t -> p (g j t)"),
             )
 
-        out_rows = out.rearrange("b (m p) h w -> b p m (h w)", p=P)
+        out_rows = out.rearrange("b (i p e) h w -> b i e p (h w)", p=P, e=PAIR)
 
         def compute_out(c, m):
             y_ps = y_psum.tile([P, CHUNK], F32, tag="y")
@@ -223,40 +234,43 @@ def tile_apnb_pb_t_kernel(tc, ctx_attn, feats, Ww, bw, Wo, bo, go, betao, mo, vo
                 out=y_sb[:], in_=y_ps[:], func=ACT.Relu, bias=shift[:, m : m + 1], scale=gain[:, m : m + 1]
             )
             for b, first, end, at in batch_parts(c * CHUNK, (c + 1) * CHUNK):
-                nc.sync.dma_start(out=out_rows[b][:, m, first:end], in_=y_sb[:, at : at + end - first])
+                nc.sync.dma_start(out=out_rows[b, m // PAIR, m % PAIR, :, first:end], in_=y_sb[:, at : at + end - first])
 
-        new_grouped(0)
-        new_fused(0)
+        def rows_to_columns(rows, n):
+            words_ps = ctx_psum.tile([P, P], F32, tag="ctx")
+            nc.tensor.transpose(words_ps[:], rows[:].bitcast(F32), ident_f32[:])
+            words = keep.tile([P, n], F32, name="words%d" % n)
+            nc.vector.tensor_copy(out=words[:], in_=words_ps[:, :n])
+            return words[:].bitcast(BF16)
+
         regroup_feats(nc.scalar.copy, 0)
+        bw_sb = rows_to_columns(bw_rows, 2)
         for j in range(SUBS):
             compute_ctx_bank(j)
+        new_fused(0)
+        quantise_fused(0, 1, 2)
+        compute_ctx_bank(SUBS)
+        quantise_fused(0, 0, 1)
+        compute_ctx_bank(SUBS + 1)
 
-        columns_ps = ctx_psum.tile([P, P], BF16, tag="ctx")
-        nc.tensor.transpose(columns_ps[:], vector_rows[:], ident_bf16[:])
-        columns = keep.tile([P, VECTORS, M_TILES], F32)
-        nc.vector.tensor_copy(
-            out=columns[:].rearrange("p v m -> p (v m)"), in_=columns_ps[:, : VECTORS * M_TILES]
-        )
         gain = keep.tile([P, M_TILES], F32)
         shift = keep.tile([P, M_TILES], F32)
-        nc.gpsimd.tensor_scalar_add(out=gain[:], in0=columns[:, 0, :], scalar1=EPS)
-        nc.gpsimd.tensor_sub(out=shift[:], in0=columns[:, 2, :], in1=columns[:, 3, :])
-
-        def finish_norm():
-            nc.scalar.activation(out=gain[:], in_=gain[:], func=ACT.Abs_reciprocal_sqrt)
-            nc.gpsimd.tensor_mul(out=gain[:], in0=gain[:], in1=columns[:, 1, :])
-            nc.gpsimd.tensor_mul(out=shift[:], in0=shift[:], in1=gain[:])
-            nc.gpsimd.tensor_add(out=shift[:], in0=shift[:], in1=columns[:, 4, :])
-
-        quantise_fused(0, 1, 2)
-        quantise_fused(0, 0, 1)
-        new_grouped(1)
-        for i in range(SUBS):
-            prepare_wo(2 * i)
-            prepare_wo(2 * i + 1)
-            compute_ctx_bank(SUBS + i)
+        for i in range(M_PAIRS):
+            for m in range(PAIR * i, PAIR * (i + 1)):
+                prepare_wo(m)
+            compute_ctx_bank(SUBS + 2 + i)
             if i == 1:
-                finish_norm()
+                columns = rows_to_columns(vector_rows, 5 * M_PAIRS)
+                vo_sb, go_sb, bo_sb, mo_sb, betao_sb = [
+                    columns[:, v * M_TILES : (v + 1) * M_TILES] for v in range(5)
+                ]
+                nc.gpsimd.tensor_scalar_add(out=gain[:], in0=vo_sb, scalar1=EPS)
+                nc.gpsimd.tensor_sub(out=shift[:], in0=bo_sb, in1=mo_sb)
+            if i == 2:
+                nc.scalar.activation(out=gain[:], in_=gain[:], func=ACT.Abs_reciprocal_sqrt)
+                nc.gpsimd.tensor_mul(out=gain[:], in0=gain[:], in1=go_sb)
+                nc.gpsimd.tensor_mul(out=shift[:], in0=shift[:], in1=gain[:])
+                nc.gpsimd.tensor_add(out=shift[:], in0=shift[:], in1=betao_sb)
         regroup_feats(nc.vector.tensor_copy, 1)
 
         new_fused(1)
@@ -264,17 +278,15 @@ def tile_apnb_pb_t_kernel(tc, ctx_attn, feats, Ww, bw, Wo, bo, go, betao, mo, vo
             compute_out(0, m)
             if m == M_TILES // 2:
                 quantise_fused(1)
-        new_grouped(2)
         regroup_feats(nc.vector.tensor_copy, 2)
 
         for c in range(1, N_CHUNKS):
+            for j in range(banks_by(c - 1), banks_by(c)):
+                compute_ctx_bank(j)
             if c + 1 < N_CHUNKS:
                 new_fused(c + 1)
-                for j in range((c + 1) * SUBS, (c + 2) * SUBS):
-                    compute_ctx_bank(j)
                 quantise_fused(c + 1)
             if c + 2 < N_CHUNKS:
-                new_grouped(c + 2)
                 regroup_feats(nc.vector.tensor_copy, c + 2)
             for m in range(M_TILES):
                 compute_out(c, m)

@@ -187,8 +187,8 @@ def tile_apnb_pb_t_kernel(tc, ctx_attn, feats, Ww, bw, Wo, bo, go, betao, mo, vo
                 )
 
         def new_fused(c):
-            codes_of[c] = fused_pool.tile([P, PASSES, CHUNK], U32, name="codes", align_bytes=64)
-            scales_of[c] = fused_pool.tile([P, PASSES, CHUNK], U8, name="scales", align_bytes=64)
+            codes_of[c] = fused_pool.tile([P, PASSES, CHUNK], U32, name="codes", align_bytes=256)
+            scales_of[c] = fused_pool.tile([P, PASSES, CHUNK], U8, name="scales", align_bytes=256)
 
         def quantise_fused(c, first=0, end=PASSES):
             nc.vector.quantize_mx(
@@ -197,8 +197,8 @@ def tile_apnb_pb_t_kernel(tc, ctx_attn, feats, Ww, bw, Wo, bo, go, betao, mo, vo
                 in_=grouped_of[c][:, first:end, :, :].rearrange("p g n t -> p (g n t)"),
             )
 
-        wo_codes = keep.tile([P, M_TILES, PASSES, P], U32, align_bytes=64)
-        wo_scales = keep.tile([P, M_TILES, PASSES, P], U8, align_bytes=64)
+        wo_codes = keep.tile([P, M_TILES, PASSES, P], U32, align_bytes=256)
+        wo_scales = keep.tile([P, M_TILES, PASSES, P], U8, align_bytes=256)
 
         def prepare_wo(m):
             words = wo_sb[:, m, :].bitcast(F32)

from contextlib import ExitStack

from concourse import mybir
from concourse.masks import make_identity

BF16 = mybir.dt.bfloat16
F32 = mybir.dt.float32
U32 = mybir.dt.uint32
U8 = mybir.dt.uint8
FP8X4 = mybir.dt.float8_e4m3fn_x4
ACT = mybir.ActivationFunctionType
ALU = mybir.AluOpType

P = 128
PACK = 4
BATCH = 2
CV = 256
C = 512
CO = 1024
HW = 48 * 48
EPS = 1e-5

POSITIONS = BATCH * HW
CHUNK = 512
N_CHUNKS = POSITIONS // CHUNK
SUB = 128
SUBS = CHUNK // SUB
K_TILES = CV // P
PASSES = 2
M_TILES = CO // P
PAIR = 2
M_PAIRS = M_TILES // PAIR
N_BANKS = POSITIONS // SUB
HEAD_BANKS = 10
PIECES = ((0, CHUNK), (CHUNK, 3 * CHUNK), (3 * CHUNK, HW), (HW, 2 * HW))


def piece_parts(lo, hi):
    parts = []
    for j, (start, end) in enumerate(PIECES):
        if max(lo, start) < min(hi, end):
            parts.append((j, max(lo, start) - start, min(hi, end) - start, max(lo, start) - lo))
    return parts


WARM_MATMULS = 3


def banks_by(c):
    return min(N_BANKS, HEAD_BANKS + -(-c * (N_BANKS - HEAD_BANKS) // (N_CHUNKS - 2)))


FLOPS = 2 * POSITIONS * (C * CV + CO * 2 * C)


def batch_parts(lo, hi):
    parts = []
    for b in range(BATCH):
        first = max(lo, b * HW)
        end = min(hi, (b + 1) * HW)
        if first < end:
            parts.append((b, first - b * HW, end - b * HW, first - lo))
    return parts


def tile_apnb_pb_t_kernel(tc, ctx_attn, feats, Ww, bw, Wo, bo, go, betao, mo, vo, out):
    nc = tc.nc
    with ExitStack() as stack:
        stack.enter_context(tc.manual_schedule())
        keep = stack.enter_context(tc.tile_pool(name="keep", bufs=1))
        wo_stage = stack.enter_context(tc.tile_pool(name="wo_stage", bufs=3))
        grouped_pool = stack.enter_context(tc.tile_pool(name="grouped_pool", bufs=4))
        fused_pool = stack.enter_context(tc.tile_pool(name="fused_pool", bufs=3))
        y_pool = stack.enter_context(tc.tile_pool(name="y_pool", bufs=24))
        ctx_psum = stack.enter_context(tc.psum_pool(name="ctx_psum", bufs=4))
        y_psum = stack.enter_context(tc.psum_pool(name="y_psum", bufs=4))

        ident_bf16 = keep.tile([P, P], BF16)
        make_identity(nc, ident_bf16[:])
        ident_f32 = keep.tile([P, P], F32)
        make_identity(nc, ident_f32[:])

        warm = keep.tile([P, 1], F32)
        nc.vector.memset(warm[:], 1.0)
        nc.scalar.activation(out=warm[:], in_=warm[:], func=ACT.Abs_reciprocal_sqrt)
        bw_rows = keep.tile([P, PAIR * P], BF16)
        nc.vector.memset(bw_rows[:], 0.0)
        vector_rows = keep.tile([P, PAIR * P], BF16)
        nc.gpsimd.memset(vector_rows[:], 0.0)
        ww_sb = keep.tile([P, PACK, CV], BF16)
        width = [end - first for first, end in PIECES]
        a_piece = [keep.tile([P, K_TILES, width[j]], BF16, name="a_piece%d" % j) for j in range(len(PIECES))]
        f_piece = [keep.tile([P, PACK, width[j]], BF16, name="f_piece%d" % j) for j in range(len(PIECES))]
        wo_sb = keep.tile([P, M_TILES, 2 * C], BF16)

        def load_ctx_attn(j):
            b, first = divmod(PIECES[j][0], HW)
            nc.sync.dma_start(
                out=a_piece[j][:],
                in_=ctx_attn[b].rearrange("(kt p) h w -> p kt (h w)", p=P)[:, :, first : first + width[j]],
            )

        def load_feats(j):
            b, first = divmod(PIECES[j][0], HW)
            rows = feats[b].rearrange("(u p e) h w -> u p e (h w)", u=2, e=2)
            for u in range(2):
                nc.sync.dma_start(
                    out=f_piece[j][:, 2 * u : 2 * u + 2, :], in_=rows[u][:, :, first : first + width[j]]
                )

        nc.sync.dma_start(
            out=ww_sb[:].rearrange("p (u e) k -> p u (e k)", u=2),
            in_=Ww.rearrange("(u p e) k -> p u (e k)", u=2, e=2),
        )
        nc.sync.dma_start(out=bw_rows[:2, :], in_=bw.rearrange("(u w) -> u w", u=2))
        load_ctx_attn(0)
        load_feats(0)
        load_ctx_attn(1)
        for i in range(M_PAIRS):
            if i == 2:
                for v, vector in enumerate((vo, go, bo, mo, betao)):
                    nc.sync.dma_start(
                        out=vector_rows[v * M_PAIRS : (v + 1) * M_PAIRS, :],
                        in_=vector.rearrange("(i w) -> i w", i=M_PAIRS),
                    )
            nc.sync.dma_start(
                out=wo_sb[:, PAIR * i : PAIR * (i + 1), :].rearrange("p e k -> p (e k)"),
                in_=Wo[PAIR * P * i : PAIR * P * (i + 1), :].rearrange("(p e) k -> p (e k)", e=PAIR),
            )
        load_feats(1)
        for j in range(2, len(PIECES)):
            load_ctx_attn(j)
            load_feats(j)

        zeros = keep.tile([P, CHUNK], BF16)
        nc.vector.memset(zeros[:], 0.0)
        idle_ps = y_psum.tile([P, CHUNK], F32, tag="y")
        for i in range(WARM_MATMULS):
            nc.tensor.matmul(out=idle_ps[:], lhsT=zeros[:, :P], rhs=zeros[:], start=True, stop=True)

        ww_t = keep.tile([P, PACK, K_TILES, P], BF16)
        for half in range(2):
            ww_t_ps = ctx_psum.tile([P, PACK // 2, K_TILES, P], BF16, tag="ctx")
            for i in range(PACK // 2):
                for kt in range(K_TILES):
                    nc.tensor.transpose(
                        ww_t_ps[:, i, kt, :],
                        ww_sb[:, half * PACK // 2 + i, kt * P : (kt + 1) * P],
                        ident_bf16[:],
                    )
            nc.vector.tensor_copy(out=ww_t[:, half * PACK // 2 : (half + 1) * PACK // 2, :, :], in_=ww_t_ps[:])

        grouped_of = {}
        codes_of = {}
        scales_of = {}

        def grouped(c):
            if c not in grouped_of:
                grouped_of[c] = grouped_pool.tile([P, PASSES, CHUNK, PACK], BF16, name="grouped", align_bytes=64)
            return grouped_of[c]

        def compute_ctx_bank(j):
            c, s = divmod(j, SUBS)
            ((piece, first, end, at),) = piece_parts(j * SUB, (j + 1) * SUB)
            ctx_ps = ctx_psum.tile([P, PACK, SUB], F32, tag="ctx")
            for t in range(PACK):
                for kt in range(K_TILES):
                    nc.tensor.matmul(
                        out=ctx_ps[:, t, :],
                        lhsT=ww_t[:, t, kt, :],
                        rhs=a_piece[piece][:, kt, first:end],
                        start=(kt == 0),
                        stop=(kt == K_TILES - 1),
                    )
            nc.vector.tensor_tensor(
                out=grouped(c)[:, 0, s * SUB : (s + 1) * SUB, :],
                in0=ctx_ps[:].rearrange("p t n -> p n t"),
                in1=bw_sb.unsqueeze(1).to_broadcast([P, SUB, PACK]),
                op=ALU.add,
            )

        def regroup_feats(copy, c):
            for piece, first, end, at in piece_parts(c * CHUNK, (c + 1) * CHUNK):
                copy(
                    out=grouped(c)[:, 1, at : at + end - first, :].rearrange("p (n i) t -> p n t i", i=4),
                    in_=f_piece[piece][:, :, first:end].rearrange("p t (n i) -> p n t i", i=4),
                )

        def new_fused(c):
            codes_of[c] = fused_pool.tile([P, PASSES, CHUNK], U32, name="codes", align_bytes=256)
            scales_of[c] = fused_pool.tile([P, PASSES, CHUNK], U8, name="scales", align_bytes=256)

        def quantise_fused(c, first=0, end=PASSES):
            nc.vector.quantize_mx(
                out=codes_of[c][:, first:end, :].rearrange("p g n -> p (g n)").bitcast(FP8X4),
                scales=scales_of[c][:, first:end, :].rearrange("p g n -> p (g n)"),
                in_=grouped_of[c][:, first:end, :, :].rearrange("p g n t -> p (g n t)"),
            )

        wo_codes = keep.tile([P, M_TILES, PASSES, P], U32, align_bytes=256)
        wo_scales = keep.tile([P, M_TILES, PASSES, P], U8, align_bytes=256)

        def prepare_wo(m):
            words = wo_sb[:, m, :].bitcast(F32)
            wo_t_ps = y_psum.tile([P, PASSES * 2, P], F32, tag="y")
            for gu in range(PASSES * 2):
                nc.tensor.transpose(wo_t_ps[:, gu, :], words[:, gu * P : (gu + 1) * P], ident_f32[:])
            wo_grouped = wo_stage.tile([P, PASSES, P, PACK], BF16, align_bytes=64)
            nc.scalar.copy(
                out=wo_grouped[:].bitcast(F32), in_=wo_t_ps[:].rearrange("p (g u) j -> p g j u", g=PASSES)
            )
            nc.vector.quantize_mx(
                out=wo_codes[:, m, :, :].rearrange("p g j -> p (g j)").bitcast(FP8X4),
                scales=wo_scales[:, m, :, :].rearrange("p g j -> p (g j)"),
                in_=wo_grouped[:].rearrange("p g j t -> p (g j t)"),
            )

        out_rows = out.rearrange("b (i p e) h w -> b i e p (h w)", p=P, e=PAIR)

        def compute_out(c, m):
            y_ps = y_psum.tile([P, CHUNK], F32, tag="y")
            for g in range(PASSES):
                nc.tensor.matmul_mx(
                    out=y_ps[:],
                    lhsT=wo_codes[:, m, g, :].bitcast(FP8X4),
                    lhsT_scale=wo_scales[:, m, g, :],
                    rhs=codes_of[c][:, g, :].bitcast(FP8X4),
                    rhs_scale=scales_of[c][:, g, :],
                    start=(g == 0),
                    stop=(g == PASSES - 1),
                )
            y_sb = y_pool.tile([P, CHUNK], F32)
            nc.scalar.activation(
                out=y_sb[:], in_=y_ps[:], func=ACT.Relu, bias=shift[:, m : m + 1], scale=gain[:, m : m + 1]
            )
            for b, first, end, at in batch_parts(c * CHUNK, (c + 1) * CHUNK):
                nc.sync.dma_start(out=out_rows[b, m // PAIR, m % PAIR, :, first:end], in_=y_sb[:, at : at + end - first])

        def rows_to_columns(rows, n):
            words_ps = ctx_psum.tile([P, P], F32, tag="ctx")
            nc.tensor.transpose(words_ps[:], rows[:].bitcast(F32), ident_f32[:])
            words = keep.tile([P, n], F32, name="words%d" % n)
            nc.vector.tensor_copy(out=words[:], in_=words_ps[:, :n])
            return words[:].bitcast(BF16)

        regroup_feats(nc.scalar.copy, 0)
        bw_sb = rows_to_columns(bw_rows, 2)
        for j in range(SUBS):
            compute_ctx_bank(j)
        new_fused(0)
        quantise_fused(0, 1, 2)
        compute_ctx_bank(SUBS)
        quantise_fused(0, 0, 1)
        compute_ctx_bank(SUBS + 1)

        gain = keep.tile([P, M_TILES], F32)
        shift = keep.tile([P, M_TILES], F32)
        for i in range(M_PAIRS):
            for m in range(PAIR * i, PAIR * (i + 1)):
                prepare_wo(m)
            compute_ctx_bank(SUBS + 2 + i)
            if i == 1:
                columns = rows_to_columns(vector_rows, 5 * M_PAIRS)
                vo_sb, go_sb, bo_sb, mo_sb, betao_sb = [
                    columns[:, v * M_TILES : (v + 1) * M_TILES] for v in range(5)
                ]
                nc.gpsimd.tensor_scalar_add(out=gain[:], in0=vo_sb, scalar1=EPS)
                nc.gpsimd.tensor_sub(out=shift[:], in0=bo_sb, in1=mo_sb)
            if i == 2:
                nc.scalar.activation(out=gain[:], in_=gain[:], func=ACT.Abs_reciprocal_sqrt)
                nc.gpsimd.tensor_mul(out=gain[:], in0=gain[:], in1=go_sb)
                nc.gpsimd.tensor_mul(out=shift[:], in0=shift[:], in1=gain[:])
                nc.gpsimd.tensor_add(out=shift[:], in0=shift[:], in1=betao_sb)
        regroup_feats(nc.vector.tensor_copy, 1)

        new_fused(1)
        for m in range(M_TILES):
            compute_out(0, m)
            if m == M_TILES // 2:
                quantise_fused(1)
        regroup_feats(nc.vector.tensor_copy, 2)

        for c in range(1, N_CHUNKS):
            for j in range(banks_by(c - 1), banks_by(c)):
                compute_ctx_bank(j)
            if c + 1 < N_CHUNKS:
                new_fused(c + 1)
                quantise_fused(c + 1)
            if c + 2 < N_CHUNKS:
                regroup_feats(nc.vector.tensor_copy, c + 2)
            for m in range(M_TILES):
                compute_out(c, m)
